import numpy as np
import ml_dtypes

BF16 = ml_dtypes.bfloat16


def bf(x):
    return np.asarray(x, np.float32).astype(BF16)


def f32(x):
    return np.asarray(x, np.float32)


def f64(x):
    return np.asarray(x).astype(np.float64)


def striped(idx):
    return np.tile(idx.reshape(-1, 16).T, (8, 1))


C, H, DK, S, N = 512, 4, 128, 2048, 512
XMAX, TMAX = 3.0, 1.5


def setup_inputs():
    return {"base": f32(np.random.standard_normal((C, S))), "x": f32(np.clip(np.random.standard_normal((C, N)), -XMAX, XMAX)), "theta": f32(np.random.uniform(-TMAX, TMAX, (DK, 1))), "w": bf(np.random.standard_normal((C, C)) / np.sqrt(C)), "offs": striped(np.random.permutation(S)[:N])}


def reference(base, x, theta, w, offs):
    idx = offs[:16].T.reshape(-1)
    xx = f64(x)
    meas = np.cos(xx + np.tile(f64(theta), (H, 1)))
    out = f64(base).copy()
    out[:, idx] = xx + f64(w).T @ meas
    return out

@@ -1,0 +1,61 @@
+import math
+
+import concourse.mybir as mybir
+
+F32 = mybir.dt.float32
+BF16 = mybir.dt.bfloat16
+U16 = mybir.dt.uint16
+
+P = 128
+C = 512
+S = 2048
+N = 512
+BLOCKS = C // P
+
+FLOPS = 2 * C * C * N
+
+
+def tile_transformerblockquantum_kernel(tc, base, x, theta, w, offs, out):
+    nc = tc.nc
+    add = mybir.AluOpType.add
+    absolute = mybir.ActivationFunctionType.Abs
+    sine = mybir.ActivationFunctionType.Sin
+
+    with tc.tile_pool(name="held", bufs=1) as held, tc.psum_pool(name="psum", bufs=1) as psum:
+        offsets = held.tile([P, N // 16], U16, name="offsets")
+        nc.sync.dma_start(offsets[:], offs)
+        angles = held.tile([P, 1], F32, name="angles")
+        nc.scalar.dma_start(angles[:], theta)
+
+        tokens = [held.tile([P, N], F32, name=f"tokens{k}") for k in range(BLOCKS)]
+        for k in range(BLOCKS):
+            nc.sync.dma_start(tokens[k][:], x[k * P : (k + 1) * P, :])
+        weights = [held.tile([P, C], BF16, name=f"weights{k}") for k in range(BLOCKS)]
+        for k in range(BLOCKS):
+            nc.sync.dma_start(weights[k][:], w[k * P : (k + 1) * P, :])
+        windows = [held.tile([P, S], F32, name=f"window{c}") for c in range(BLOCKS)]
+        for c in range(BLOCKS):
+            nc.sync.dma_start(windows[c][:], base[c * P : (c + 1) * P, :])
+
+        half_pi = held.tile([P, 1], F32, name="half_pi")
+        nc.vector.memset(half_pi[:], math.pi / 2)
+        measured = [held.tile([P, N], BF16, name=f"measured{k}") for k in range(BLOCKS)]
+        products = [psum.tile([P, N], F32, name=f"product{c}") for c in range(BLOCKS)]
+        for k in range(BLOCKS):
+            size = held.tile([P, N], F32, name=f"size{k}")
+            nc.scalar.activation(size[:], tokens[k][:], absolute, bias=angles[:], scale=1.0)
+            nc.scalar.activation(measured[k][:], size[:], sine, bias=half_pi[:], scale=-1.0)
+            for c in range(BLOCKS):
+                nc.tensor.matmul(
+                    products[c][:],
+                    weights[k][:, c * P : (c + 1) * P],
+                    measured[k][:],
+                    start=(k == 0),
+                    stop=(k == BLOCKS - 1),
+                )
+
+        for c in range(BLOCKS):
+            combined = held.tile([P, N], F32, name=f"combined{c}")
+            nc.scalar.copy(combined[:], products[c][:])
+            nc.vector.tensor_tensor(windows[c][:].indirect(offsets[:]), combined[:], tokens[c][:], add)
+            nc.sync.dma_start(out[c * P : (c + 1) * P, :], windows[c][:])

@@ -17,45 +17,48 @@ FLOPS = 2 * C * C * N
 
 def tile_transformerblockquantum_kernel(tc, base, x, theta, w, offs, out):
     nc = tc.nc
-    add = mybir.AluOpType.add
-    absolute = mybir.ActivationFunctionType.Abs
+    add, mult, minimum = mybir.AluOpType.add, mybir.AluOpType.mult, mybir.AluOpType.min
     sine = mybir.ActivationFunctionType.Sin
 
     with tc.tile_pool(name="held", bufs=1) as held, tc.psum_pool(name="psum", bufs=1) as psum:
         offsets = held.tile([P, N // 16], U16, name="offsets")
         nc.sync.dma_start(offsets[:], offs)
         angles = held.tile([P, 1], F32, name="angles")
-        nc.scalar.dma_start(angles[:], theta)
+        nc.gpsimd.dma_start(angles[:], theta)
 
         tokens = [held.tile([P, N], F32, name=f"tokens{k}") for k in range(BLOCKS)]
         for k in range(BLOCKS):
             nc.sync.dma_start(tokens[k][:], x[k * P : (k + 1) * P, :])
-        weights = [held.tile([P, C], BF16, name=f"weights{k}") for k in range(BLOCKS)]
-        for k in range(BLOCKS):
-            nc.sync.dma_start(weights[k][:], w[k * P : (k + 1) * P, :])
+        weights = held.tile([P, BLOCKS, C], BF16, name="weights")
+        nc.sync.dma_start(weights[:], w.rearrange("(k p) c -> p k c", p=P))
         windows = [held.tile([P, S], F32, name=f"window{c}") for c in range(BLOCKS)]
         for c in range(BLOCKS):
             nc.sync.dma_start(windows[c][:], base[c * P : (c + 1) * P, :])
 
         half_pi = held.tile([P, 1], F32, name="half_pi")
         nc.vector.memset(half_pi[:], math.pi / 2)
+        warmed = held.tile([P, 1], F32, name="warmed")
+        nc.scalar.activation(warmed[:], half_pi[:], sine)
+
         measured = [held.tile([P, N], BF16, name=f"measured{k}") for k in range(BLOCKS)]
-        products = [psum.tile([P, N], F32, name=f"product{c}") for c in range(BLOCKS)]
         for k in range(BLOCKS):
-            size = held.tile([P, N], F32, name=f"size{k}")
-            nc.scalar.activation(size[:], tokens[k][:], absolute, bias=angles[:], scale=1.0)
-            nc.scalar.activation(measured[k][:], size[:], sine, bias=half_pi[:], scale=-1.0)
-            for c in range(BLOCKS):
+            negated = held.tile([P, N], F32, name=f"negated{k}")
+            nc.vector.tensor_scalar(negated[:], tokens[k][:], angles[:], -1.0, add, mult)
+            folded = held.tile([P, N], F32, name=f"folded{k}")
+            nc.vector.scalar_tensor_tensor(folded[:], negated[:], -1.0, negated[:], mult, minimum)
+            nc.scalar.activation(measured[k][:], folded[:], sine, bias=half_pi[:], scale=1.0)
+
+        for c in range(BLOCKS):
+            product = psum.tile([P, N], F32, name="product")
+            for k in range(BLOCKS):
                 nc.tensor.matmul(
-                    products[c][:],
-                    weights[k][:, c * P : (c + 1) * P],
+                    product[:],
+                    weights[:, k, c * P : (c + 1) * P],
                     measured[k][:],
                     start=(k == 0),
                     stop=(k == BLOCKS - 1),
                 )
-
-        for c in range(BLOCKS):
             combined = held.tile([P, N], F32, name=f"combined{c}")
-            nc.scalar.copy(combined[:], products[c][:])
+            nc.scalar.copy(combined[:], product[:])
             nc.vector.tensor_tensor(windows[c][:].indirect(offsets[:]), combined[:], tokens[c][:], add)
             nc.sync.dma_start(out[c * P : (c + 1) * P, :], windows[c][:])

@@ -24,7 +24,7 @@ def tile_transformerblockquantum_kernel(tc, base, x, theta, w, offs, out):
         offsets = held.tile([P, N // 16], U16, name="offsets")
         nc.sync.dma_start(offsets[:], offs)
         angles = held.tile([P, 1], F32, name="angles")
-        nc.gpsimd.dma_start(angles[:], theta)
+        nc.scalar.dma_start(angles[:], theta)
 
         tokens = [held.tile([P, N], F32, name=f"tokens{k}") for k in range(BLOCKS)]
         for k in range(BLOCKS):

@@ -17,7 +17,8 @@ FLOPS = 2 * C * C * N
 
 def tile_transformerblockquantum_kernel(tc, base, x, theta, w, offs, out):
     nc = tc.nc
-    add, mult, minimum = mybir.AluOpType.add, mybir.AluOpType.mult, mybir.AluOpType.min
+    add, mult, maximum = mybir.AluOpType.add, mybir.AluOpType.mult, mybir.AluOpType.max
+    absolute = mybir.ActivationFunctionType.Abs
     sine = mybir.ActivationFunctionType.Sin
 
     with tc.tile_pool(name="held", bufs=1) as held, tc.psum_pool(name="psum", bufs=1) as psum:
@@ -42,11 +43,14 @@ def tile_transformerblockquantum_kernel(tc, base, x, theta, w, offs, out):
 
         measured = [held.tile([P, N], BF16, name=f"measured{k}") for k in range(BLOCKS)]
         for k in range(BLOCKS):
-            negated = held.tile([P, N], F32, name=f"negated{k}")
-            nc.vector.tensor_scalar(negated[:], tokens[k][:], angles[:], -1.0, add, mult)
             folded = held.tile([P, N], F32, name=f"folded{k}")
-            nc.vector.scalar_tensor_tensor(folded[:], negated[:], -1.0, negated[:], mult, minimum)
-            nc.scalar.activation(measured[k][:], folded[:], sine, bias=half_pi[:], scale=1.0)
+            if k % 2 == 0:
+                nc.scalar.activation(folded[:], tokens[k][:], absolute, bias=angles[:], scale=1.0)
+            else:
+                negated = held.tile([P, N], F32, name=f"negated{k}")
+                nc.vector.tensor_scalar(negated[:], tokens[k][:], angles[:], -1.0, add, mult)
+                nc.vector.scalar_tensor_tensor(folded[:], negated[:], -1.0, negated[:], mult, maximum)
+            nc.scalar.activation(measured[k][:], folded[:], sine, bias=half_pi[:], scale=-1.0)
 
         for c in range(BLOCKS):
             product = psum.tile([P, N], F32, name="product")

@@ -22,18 +22,17 @@ def tile_transformerblockquantum_kernel(tc, base, x, theta, w, offs, out):
     sine = mybir.ActivationFunctionType.Sin
 
     with tc.tile_pool(name="held", bufs=1) as held, tc.psum_pool(name="psum", bufs=1) as psum:
-        offsets = held.tile([P, N // 16], U16, name="offsets")
-        nc.sync.dma_start(offsets[:], offs)
         angles = held.tile([P, 1], F32, name="angles")
         nc.scalar.dma_start(angles[:], theta)
-
         tokens = [held.tile([P, N], F32, name=f"tokens{k}") for k in range(BLOCKS)]
         for k in range(BLOCKS):
             nc.sync.dma_start(tokens[k][:], x[k * P : (k + 1) * P, :])
-        weights = held.tile([P, BLOCKS, C], BF16, name="weights")
-        nc.sync.dma_start(weights[:], w.rearrange("(k p) c -> p k c", p=P))
+        offsets = held.tile([P, N // 16], U16, name="offsets")
+        nc.sync.dma_start(offsets[:], offs)
+        weights = [held.tile([P, BLOCKS, P], BF16, name=f"weights{c}") for c in range(BLOCKS)]
         windows = [held.tile([P, S], F32, name=f"window{c}") for c in range(BLOCKS)]
         for c in range(BLOCKS):
+            nc.sync.dma_start(weights[c][:], w[:, c * P : (c + 1) * P].rearrange("(k p) c -> p k c", p=P))
             nc.sync.dma_start(windows[c][:], base[c * P : (c + 1) * P, :])
 
         half_pi = held.tile([P, 1], F32, name="half_pi")
@@ -57,7 +56,7 @@ def tile_transformerblockquantum_kernel(tc, base, x, theta, w, offs, out):
             for k in range(BLOCKS):
                 nc.tensor.matmul(
                     product[:],
-                    weights[:, k, c * P : (c + 1) * P],
+                    weights[c][:, k, :],
                     measured[k][:],
                     start=(k == 0),
                     stop=(k == BLOCKS - 1),

@@ -12,6 +12,8 @@ S = 2048
 N = 512
 BLOCKS = C // P
 
+WARMING_MATMULS = 8
+
 FLOPS = 2 * C * C * N
 
 
@@ -39,6 +41,12 @@ def tile_transformerblockquantum_kernel(tc, base, x, theta, w, offs, out):
         nc.vector.memset(half_pi[:], math.pi / 2)
         warmed = held.tile([P, 1], F32, name="warmed")
         nc.scalar.activation(warmed[:], half_pi[:], sine)
+
+        zeros = held.tile([P, N], BF16, name="zeros")
+        nc.gpsimd.memset(zeros[:], 0.0)
+        unread = psum.tile([P, N], F32, name="unread")
+        for i in range(WARMING_MATMULS):
+            nc.tensor.matmul(unread[:], zeros[:, 0:P], zeros[:], start=True, stop=True)
 
         measured = [held.tile([P, N], BF16, name=f"measured{k}") for k in range(BLOCKS)]
         for k in range(BLOCKS):

@@ -11,6 +11,12 @@ C = 512
 S = 2048
 N = 512
 BLOCKS = C // P
+HALVES = 2
+
+
+def half(h):
+    return slice(h * (N // HALVES), (h + 1) * (N // HALVES))
+
 
 WARMING_MATMULS = 8
 
@@ -57,19 +63,30 @@ def tile_transformerblockquantum_kernel(tc, base, x, theta, w, offs, out):
                 negated = held.tile([P, N], F32, name=f"negated{k}")
                 nc.vector.tensor_scalar(negated[:], tokens[k][:], angles[:], -1.0, add, mult)
                 nc.vector.scalar_tensor_tensor(folded[:], negated[:], -1.0, negated[:], mult, maximum)
-            nc.scalar.activation(measured[k][:], folded[:], sine, bias=half_pi[:], scale=-1.0)
+            if k < BLOCKS - 1:
+                nc.scalar.activation(measured[k][:], folded[:], sine, bias=half_pi[:], scale=-1.0)
+            else:
+                for h in range(HALVES):
+                    nc.scalar.activation(
+                        measured[k][:, half(h)], folded[:, half(h)], sine, bias=half_pi[:], scale=-1.0
+                    )
 
         for c in range(BLOCKS):
-            product = psum.tile([P, N], F32, name="product")
+            products = [psum.tile([P, N // HALVES], F32, name=f"product{h}") for h in range(HALVES)]
             for k in range(BLOCKS):
-                nc.tensor.matmul(
-                    product[:],
-                    weights[c][:, k, :],
-                    measured[k][:],
-                    start=(k == 0),
-                    stop=(k == BLOCKS - 1),
-                )
+                for h in range(HALVES):
+                    nc.tensor.matmul(
+                        products[h][:],
+                        weights[c][:, k, :],
+                        measured[k][:, half(h)],
+                        start=(k == 0),
+                        stop=(k == BLOCKS - 1),
+                    )
             combined = held.tile([P, N], F32, name=f"combined{c}")
-            nc.scalar.copy(combined[:], product[:])
+            for h in range(HALVES):
+                if c == 0:
+                    nc.vector.tensor_copy(combined[:, half(h)], products[h][:])
+                else:
+                    nc.scalar.copy(combined[:, half(h)], products[h][:])
             nc.vector.tensor_tensor(windows[c][:].indirect(offsets[:]), combined[:], tokens[c][:], add)
             nc.sync.dma_start(out[c * P : (c + 1) * P, :], windows[c][:])

@@ -37,10 +37,13 @@ def tile_transformerblockquantum_kernel(tc, base, x, theta, w, offs, out):
             nc.sync.dma_start(tokens[k][:], x[k * P : (k + 1) * P, :])
         offsets = held.tile([P, N // 16], U16, name="offsets")
         nc.sync.dma_start(offsets[:], offs)
-        weights = [held.tile([P, BLOCKS, P], BF16, name=f"weights{c}") for c in range(BLOCKS)]
+        first_weights = held.tile([P, BLOCKS, P], BF16, name="first_weights")
+        later_weights = held.tile([P, BLOCKS, C - P], BF16, name="later_weights")
         windows = [held.tile([P, S], F32, name=f"window{c}") for c in range(BLOCKS)]
-        for c in range(BLOCKS):
-            nc.sync.dma_start(weights[c][:], w[:, c * P : (c + 1) * P].rearrange("(k p) c -> p k c", p=P))
+        nc.sync.dma_start(first_weights[:], w[:, 0:P].rearrange("(k p) c -> p k c", p=P))
+        nc.sync.dma_start(windows[0][:], base[0:P, :])
+        nc.sync.dma_start(later_weights[:], w[:, P:C].rearrange("(k p) c -> p k c", p=P))
+        for c in range(1, BLOCKS):
             nc.sync.dma_start(windows[c][:], base[c * P : (c + 1) * P, :])
 
         half_pi = held.tile([P, 1], F32, name="half_pi")
@@ -77,7 +80,7 @@ def tile_transformerblockquantum_kernel(tc, base, x, theta, w, offs, out):
                 for h in range(HALVES):
                     nc.tensor.matmul(
                         products[h][:],
-                        weights[c][:, k, :],
+                        first_weights[:, k, :] if c == 0 else later_weights[:, k, (c - 1) * P : c * P],
                         measured[k][:, half(h)],
                         start=(k == 0),
                         stop=(k == BLOCKS - 1),

@@ -61,18 +61,20 @@ def tile_transformerblockquantum_kernel(tc, base, x, theta, w, offs, out):
         for k in range(BLOCKS):
             folded = held.tile([P, N], F32, name=f"folded{k}")
             if k % 2 == 0:
-                nc.scalar.activation(folded[:], tokens[k][:], absolute, bias=angles[:], scale=1.0)
-            else:
-                negated = held.tile([P, N], F32, name=f"negated{k}")
-                nc.vector.tensor_scalar(negated[:], tokens[k][:], angles[:], -1.0, add, mult)
-                nc.vector.scalar_tensor_tensor(folded[:], negated[:], -1.0, negated[:], mult, maximum)
-            if k < BLOCKS - 1:
-                nc.scalar.activation(measured[k][:], folded[:], sine, bias=half_pi[:], scale=-1.0)
-            else:
                 for h in range(HALVES):
                     nc.scalar.activation(
-                        measured[k][:, half(h)], folded[:, half(h)], sine, bias=half_pi[:], scale=-1.0
+                        folded[:, half(h)], tokens[k][:, half(h)], absolute, bias=angles[:], scale=1.0
                     )
+            else:
+                negated = held.tile([P, N], F32, name=f"negated{k}")
+                for h in range(HALVES):
+                    nc.vector.tensor_scalar(negated[:, half(h)], tokens[k][:, half(h)], angles[:], -1.0, add, mult)
+                for h in range(HALVES):
+                    nc.vector.scalar_tensor_tensor(
+                        folded[:, half(h)], negated[:, half(h)], -1.0, negated[:, half(h)], mult, maximum
+                    )
+            for h in range(HALVES):
+                nc.scalar.activation(measured[k][:, half(h)], folded[:, half(h)], sine, bias=half_pi[:], scale=-1.0)
 
         for c in range(BLOCKS):
             products = [psum.tile([P, N // HALVES], F32, name=f"product{h}") for h in range(HALVES)]

@@ -5,6 +5,7 @@ import concourse.mybir as mybir
 F32 = mybir.dt.float32
 BF16 = mybir.dt.bfloat16
 U16 = mybir.dt.uint16
+I32 = mybir.dt.int32
 
 P = 128
 C = 512
@@ -20,12 +21,14 @@ def half(h):
 
 WARMING_MATMULS = 8
 
+ALL_BUT_SIGN = 0x7FFFFFFF
+
 FLOPS = 2 * C * C * N
 
 
 def tile_transformerblockquantum_kernel(tc, base, x, theta, w, offs, out):
     nc = tc.nc
-    add, mult, maximum = mybir.AluOpType.add, mybir.AluOpType.mult, mybir.AluOpType.max
+    add, bitwise_and = mybir.AluOpType.add, mybir.AluOpType.bitwise_and
     absolute = mybir.ActivationFunctionType.Abs
     sine = mybir.ActivationFunctionType.Sin
 
@@ -60,18 +63,22 @@ def tile_transformerblockquantum_kernel(tc, base, x, theta, w, offs, out):
         measured = [held.tile([P, N], BF16, name=f"measured{k}") for k in range(BLOCKS)]
         for k in range(BLOCKS):
             folded = held.tile([P, N], F32, name=f"folded{k}")
-            if k % 2 == 0:
+            if k == 0:
                 for h in range(HALVES):
                     nc.scalar.activation(
                         folded[:, half(h)], tokens[k][:, half(h)], absolute, bias=angles[:], scale=1.0
                     )
             else:
-                negated = held.tile([P, N], F32, name=f"negated{k}")
+                argument = held.tile([P, N], F32, name=f"argument{k}")
                 for h in range(HALVES):
-                    nc.vector.tensor_scalar(negated[:, half(h)], tokens[k][:, half(h)], angles[:], -1.0, add, mult)
+                    nc.vector.tensor_scalar(argument[:, half(h)], tokens[k][:, half(h)], angles[:], None, add)
                 for h in range(HALVES):
-                    nc.vector.scalar_tensor_tensor(
-                        folded[:, half(h)], negated[:, half(h)], -1.0, negated[:, half(h)], mult, maximum
+                    nc.vector.tensor_scalar(
+                        folded[:, half(h)].bitcast(I32),
+                        argument[:, half(h)].bitcast(I32),
+                        ALL_BUT_SIGN,
+                        None,
+                        bitwise_and,
                     )
             for h in range(HALVES):
                 nc.scalar.activation(measured[k][:, half(h)], folded[:, half(h)], sine, bias=half_pi[:], scale=-1.0)

@@ -35,15 +35,15 @@ def tile_transformerblockquantum_kernel(tc, base, x, theta, w, offs, out):
     with tc.tile_pool(name="held", bufs=1) as held, tc.psum_pool(name="psum", bufs=1) as psum:
         angles = held.tile([P, 1], F32, name="angles")
         nc.scalar.dma_start(angles[:], theta)
+        first_weights = held.tile([P, BLOCKS, P], BF16, name="first_weights")
+        nc.scalar.dma_start(first_weights[:], w[:, 0:P].rearrange("(k p) c -> p k c", p=P))
         tokens = [held.tile([P, N], F32, name=f"tokens{k}") for k in range(BLOCKS)]
         for k in range(BLOCKS):
             nc.sync.dma_start(tokens[k][:], x[k * P : (k + 1) * P, :])
         offsets = held.tile([P, N // 16], U16, name="offsets")
         nc.sync.dma_start(offsets[:], offs)
-        first_weights = held.tile([P, BLOCKS, P], BF16, name="first_weights")
         later_weights = held.tile([P, BLOCKS, C - P], BF16, name="later_weights")
         windows = [held.tile([P, S], F32, name=f"window{c}") for c in range(BLOCKS)]
-        nc.sync.dma_start(first_weights[:], w[:, 0:P].rearrange("(k p) c -> p k c", p=P))
         nc.sync.dma_start(windows[0][:], base[0:P, :])
         nc.sync.dma_start(later_weights[:], w[:, P:C].rearrange("(k p) c -> p k c", p=P))
         for c in range(1, BLOCKS):

@@ -12,6 +12,7 @@ C = 512
 S = 2048
 N = 512
 BLOCKS = C // P
+DMA_ALIGNMENT = 256
 HALVES = 2
 
 
@@ -35,15 +36,17 @@ def tile_transformerblockquantum_kernel(tc, base, x, theta, w, offs, out):
     with tc.tile_pool(name="held", bufs=1) as held, tc.psum_pool(name="psum", bufs=1) as psum:
         angles = held.tile([P, 1], F32, name="angles")
         nc.scalar.dma_start(angles[:], theta)
-        first_weights = held.tile([P, BLOCKS, P], BF16, name="first_weights")
+        first_weights = held.tile([P, BLOCKS, P], BF16, name="first_weights", align_bytes=DMA_ALIGNMENT)
         nc.scalar.dma_start(first_weights[:], w[:, 0:P].rearrange("(k p) c -> p k c", p=P))
-        tokens = [held.tile([P, N], F32, name=f"tokens{k}") for k in range(BLOCKS)]
+        tokens = [held.tile([P, N], F32, name=f"tokens{k}", align_bytes=DMA_ALIGNMENT) for k in range(BLOCKS)]
         for k in range(BLOCKS):
             nc.sync.dma_start(tokens[k][:], x[k * P : (k + 1) * P, :])
         offsets = held.tile([P, N // 16], U16, name="offsets")
         nc.sync.dma_start(offsets[:], offs)
-        later_weights = held.tile([P, BLOCKS, C - P], BF16, name="later_weights")
-        windows = [held.tile([P, S], F32, name=f"window{c}") for c in range(BLOCKS)]
+        later_weights = held.tile([P, BLOCKS, C - P], BF16, name="later_weights", align_bytes=DMA_ALIGNMENT)
+        windows = [
+            held.tile([P, S], F32, name=f"window{c}", align_bytes=DMA_ALIGNMENT) for c in range(BLOCKS)
+        ]
         nc.sync.dma_start(windows[0][:], base[0:P, :])
         nc.sync.dma_start(later_weights[:], w[:, P:C].rearrange("(k p) c -> p k c", p=P))
         for c in range(1, BLOCKS):

@@ -66,23 +66,23 @@ def tile_transformerblockquantum_kernel(tc, base, x, theta, w, offs, out):
         measured = [held.tile([P, N], BF16, name=f"measured{k}") for k in range(BLOCKS)]
         for k in range(BLOCKS):
             folded = held.tile([P, N], F32, name=f"folded{k}")
-            if k == 0:
-                for h in range(HALVES):
-                    nc.scalar.activation(
-                        folded[:, half(h)], tokens[k][:, half(h)], absolute, bias=angles[:], scale=1.0
-                    )
-            else:
-                argument = held.tile([P, N], F32, name=f"argument{k}")
-                for h in range(HALVES):
-                    nc.vector.tensor_scalar(argument[:, half(h)], tokens[k][:, half(h)], angles[:], None, add)
-                for h in range(HALVES):
-                    nc.vector.tensor_scalar(
-                        folded[:, half(h)].bitcast(I32),
-                        argument[:, half(h)].bitcast(I32),
-                        ALL_BUT_SIGN,
-                        None,
-                        bitwise_and,
-                    )
+            argument = held.tile([P, N], F32, name=f"argument{k}")
+            by_scalar = {0: [0], BLOCKS - 1: [1]}.get(k, [])
+            by_vector = [h for h in range(HALVES) if h not in by_scalar]
+            for h in by_scalar:
+                nc.scalar.activation(
+                    folded[:, half(h)], tokens[k][:, half(h)], absolute, bias=angles[:], scale=1.0
+                )
+            for h in by_vector:
+                nc.vector.tensor_scalar(argument[:, half(h)], tokens[k][:, half(h)], angles[:], None, add)
+            for h in by_vector:
+                nc.vector.tensor_scalar(
+                    folded[:, half(h)].bitcast(I32),
+                    argument[:, half(h)].bitcast(I32),
+                    ALL_BUT_SIGN,
+                    None,
+                    bitwise_and,
+                )
             for h in range(HALVES):
                 nc.scalar.activation(measured[k][:, half(h)], folded[:, half(h)], sine, bias=half_pi[:], scale=-1.0)
 

@@ -36,8 +36,6 @@ def tile_transformerblockquantum_kernel(tc, base, x, theta, w, offs, out):
     with tc.tile_pool(name="held", bufs=1) as held, tc.psum_pool(name="psum", bufs=1) as psum:
         angles = held.tile([P, 1], F32, name="angles")
         nc.scalar.dma_start(angles[:], theta)
-        first_weights = held.tile([P, BLOCKS, P], BF16, name="first_weights", align_bytes=DMA_ALIGNMENT)
-        nc.scalar.dma_start(first_weights[:], w[:, 0:P].rearrange("(k p) c -> p k c", p=P))
         tokens = [held.tile([P, N], F32, name=f"tokens{k}", align_bytes=DMA_ALIGNMENT) for k in range(BLOCKS)]
         for k in range(BLOCKS):
             nc.sync.dma_start(tokens[k][:], x[k * P : (k + 1) * P, :])
@@ -56,6 +54,9 @@ def tile_transformerblockquantum_kernel(tc, base, x, theta, w, offs, out):
         nc.vector.memset(half_pi[:], math.pi / 2)
         warmed = held.tile([P, 1], F32, name="warmed")
         nc.scalar.activation(warmed[:], half_pi[:], sine)
+
+        first_weights = held.tile([P, BLOCKS, P], BF16, name="first_weights", align_bytes=DMA_ALIGNMENT)
+        nc.scalar.dma_start(first_weights[:], w[:, 0:P].rearrange("(k p) c -> p k c", p=P))
 
         zeros = held.tile([P, N], BF16, name="zeros")
         nc.gpsimd.memset(zeros[:], 0.0)

import math

import concourse.mybir as mybir

F32 = mybir.dt.float32
BF16 = mybir.dt.bfloat16
U16 = mybir.dt.uint16
I32 = mybir.dt.int32

P = 128
C = 512
S = 2048
N = 512
BLOCKS = C // P
DMA_ALIGNMENT = 256
HALVES = 2


def half(h):
    return slice(h * (N // HALVES), (h + 1) * (N // HALVES))


WARMING_MATMULS = 8

ALL_BUT_SIGN = 0x7FFFFFFF

FLOPS = 2 * C * C * N


def tile_transformerblockquantum_kernel(tc, base, x, theta, w, offs, out):
    nc = tc.nc
    add, bitwise_and = mybir.AluOpType.add, mybir.AluOpType.bitwise_and
    absolute = mybir.ActivationFunctionType.Abs
    sine = mybir.ActivationFunctionType.Sin

    with tc.tile_pool(name="held", bufs=1) as held, tc.psum_pool(name="psum", bufs=1) as psum:
        angles = held.tile([P, 1], F32, name="angles")
        nc.scalar.dma_start(angles[:], theta)
        tokens = [held.tile([P, N], F32, name=f"tokens{k}", align_bytes=DMA_ALIGNMENT) for k in range(BLOCKS)]
        for k in range(BLOCKS):
            nc.sync.dma_start(tokens[k][:], x[k * P : (k + 1) * P, :])
        offsets = held.tile([P, N // 16], U16, name="offsets")
        nc.sync.dma_start(offsets[:], offs)
        later_weights = held.tile([P, BLOCKS, C - P], BF16, name="later_weights", align_bytes=DMA_ALIGNMENT)
        windows = [
            held.tile([P, S], F32, name=f"window{c}", align_bytes=DMA_ALIGNMENT) for c in range(BLOCKS)
        ]
        nc.sync.dma_start(windows[0][:], base[0:P, :])
        nc.sync.dma_start(later_weights[:], w[:, P:C].rearrange("(k p) c -> p k c", p=P))
        for c in range(1, BLOCKS):
            nc.sync.dma_start(windows[c][:], base[c * P : (c + 1) * P, :])

        half_pi = held.tile([P, 1], F32, name="half_pi")
        nc.vector.memset(half_pi[:], math.pi / 2)
        warmed = held.tile([P, 1], F32, name="warmed")
        nc.scalar.activation(warmed[:], half_pi[:], sine)

        first_weights = held.tile([P, BLOCKS, P], BF16, name="first_weights", align_bytes=DMA_ALIGNMENT)
        nc.scalar.dma_start(first_weights[:], w[:, 0:P].rearrange("(k p) c -> p k c", p=P))

        zeros = held.tile([P, N], BF16, name="zeros")
        nc.gpsimd.memset(zeros[:], 0.0)
        unread = psum.tile([P, N], F32, name="unread")
        for i in range(WARMING_MATMULS):
            nc.tensor.matmul(unread[:], zeros[:, 0:P], zeros[:], start=True, stop=True)

        measured = [held.tile([P, N], BF16, name=f"measured{k}") for k in range(BLOCKS)]
        for k in range(BLOCKS):
            folded = held.tile([P, N], F32, name=f"folded{k}")
            argument = held.tile([P, N], F32, name=f"argument{k}")
            by_scalar = {0: [0], BLOCKS - 1: [1]}.get(k, [])
            by_vector = [h for h in range(HALVES) if h not in by_scalar]
            for h in by_scalar:
                nc.scalar.activation(
                    folded[:, half(h)], tokens[k][:, half(h)], absolute, bias=angles[:], scale=1.0
                )
            for h in by_vector:
                nc.vector.tensor_scalar(argument[:, half(h)], tokens[k][:, half(h)], angles[:], None, add)
            for h in by_vector:
                nc.vector.tensor_scalar(
                    folded[:, half(h)].bitcast(I32),
                    argument[:, half(h)].bitcast(I32),
                    ALL_BUT_SIGN,
                    None,
                    bitwise_and,
                )
            for h in range(HALVES):
                nc.scalar.activation(measured[k][:, half(h)], folded[:, half(h)], sine, bias=half_pi[:], scale=-1.0)

        for c in range(BLOCKS):
            products = [psum.tile([P, N // HALVES], F32, name=f"product{h}") for h in range(HALVES)]
            for k in range(BLOCKS):
                for h in range(HALVES):
                    nc.tensor.matmul(
                        products[h][:],
                        first_weights[:, k, :] if c == 0 else later_weights[:, k, (c - 1) * P : c * P],
                        measured[k][:, half(h)],
                        start=(k == 0),
                        stop=(k == BLOCKS - 1),
                    )
            combined = held.tile([P, N], F32, name=f"combined{c}")
            for h in range(HALVES):
                if c == 0:
                    nc.vector.tensor_copy(combined[:, half(h)], products[h][:])
                else:
                    nc.scalar.copy(combined[:, half(h)], products[h][:])
            nc.vector.tensor_tensor(windows[c][:].indirect(offsets[:]), combined[:], tokens[c][:], add)
            nc.sync.dma_start(out[c * P : (c + 1) * P, :], windows[c][:])
